import numpy as np
import ml_dtypes


def mxq(x, axis, fmt="e4m3"):
    dtype, down = {"e4m3": (ml_dtypes.float8_e4m3fn, 7), "e5m2": (ml_dtypes.float8_e5m2, 14)}[fmt]
    v = np.moveaxis(np.asarray(x, np.float32).astype(ml_dtypes.bfloat16).astype(np.float64), axis, -1)
    blocks = v.reshape(v.shape[:-1] + (-1, 32))
    amax = np.abs(blocks).max(-1, keepdims=True)
    byte = np.maximum(np.where(amax > 0, np.frexp(amax)[1] - 1 + 127, 0) - down, 1)
    scale = np.exp2(byte - 127.0)
    codes = (blocks / scale).astype(np.float32).astype(dtype).astype(np.float64)
    return np.moveaxis((codes * scale).reshape(v.shape), -1, axis)


WIDE = False


def mx_kscale(k):
    if not WIDE:
        return np.ones(k)
    levels = np.array([10, -10, 5, -5, 0])
    a = np.random.permutation(np.resize(levels, k // 512 * 4)).reshape(k // 512, 4)
    idx = np.arange(k)
    return np.exp2(a[idx // 512, idx % 128 // 32])


BF16 = ml_dtypes.bfloat16


def bf(x):
    return np.asarray(x, np.float32).astype(BF16)


def f64(x):
    return np.asarray(x).astype(np.float64)


B, N, K, H, C_E, M = 2, 64, 16, 1024, 1024, 1024


def gelu_tanh(v):
    return 0.5 * v * (1.0 + np.tanh(np.sqrt(2.0 / np.pi) * (v + 0.044715 * v**3)))


def setup_inputs():
    sv, se = mx_kscale(H), mx_kscale(C_E)
    s = np.concatenate([sv, se])
    return {"h_V": bf(np.random.standard_normal((B, N, H)) * sv),
            "h_E": bf(np.random.standard_normal((B, N, K, C_E)) * se),
            "W1_w": bf(np.random.standard_normal((H + C_E, M)) / np.sqrt(H + C_E) / s[:, None]),
            "W1_b": bf(np.random.standard_normal(M) * 0.1),
            "W2_w": bf(np.random.standard_normal((M, M)) * 1.5 / np.sqrt(M)),
            "W2_b": bf(np.random.standard_normal(M) * 0.1)}


def reference(h_V, h_E, W1_w, W1_b, W2_w, W2_b):
    w1 = f64(W1_w)
    pv = mxq(f64(h_V), 2, "e4m3") @ mxq(w1[:H], 0, "e4m3")
    pe = mxq(f64(h_E), 3, "e4m3") @ mxq(w1[H:], 0, "e4m3")
    h1 = gelu_tanh(pv[:, :, None, :] + pe + f64(W1_b))
    return gelu_tanh((mxq(h1, 3, "e4m3") @ mxq(f64(W2_w), 0, "e4m3")) + f64(W2_b))

@@ -1,0 +1,253 @@
+from contextlib import ExitStack
+
+import concourse.mybir as mybir
+from concourse.masks import make_identity
+
+F32 = mybir.dt.float32
+BF16 = mybir.dt.bfloat16
+U32 = mybir.dt.uint32
+U8 = mybir.dt.uint8
+FP8X4 = mybir.dt.float8_e4m3fn_x4
+GELU = mybir.ActivationFunctionType.Gelu_apprx_tanh
+ADD = mybir.AluOpType.add
+
+P = 128
+PACK = 4
+K_PASS = P * PACK
+FEAT = 1024
+PASSES = FEAT // K_PASS
+BLOCKS = 16
+BLOCKS_PER_LOAD = 4
+BANK = 512
+TURN = 2
+LEAD = 3
+
+FLOPS = 2 * (P * FEAT * FEAT + 2 * P * BLOCKS * FEAT * FEAT)
+
+
+def tile_declayerj_pa_kernel(tc, h_V, h_E, W1_w, W1_b, W2_w, W2_b, out):
+    nc = tc.nc
+    node_rows = h_V.rearrange("b n c -> (b n) c")
+    edge_rows = h_E.rearrange("b n k c -> (b n) k c")
+    out_rows = out.rearrange("b n k m -> (b n) k m")
+
+    with ExitStack() as ctx:
+        keep = ctx.enter_context(tc.tile_pool(name="keep", bufs=1))
+        edges_in = ctx.enter_context(tc.tile_pool(name="edges_in", bufs=BLOCKS // BLOCKS_PER_LOAD))
+        weights_in = ctx.enter_context(tc.tile_pool(name="weights_in", bufs=3 * PASSES))
+        regrouped = ctx.enter_context(tc.tile_pool(name="regrouped", bufs=2))
+        stream = ctx.enter_context(tc.tile_pool(name="stream", bufs=3))
+        psum = ctx.enter_context(tc.psum_pool(name="psum", bufs=8))
+
+        ident = keep.tile([P, P], F32, name="ident")
+        make_identity(nc, ident[:])
+        warm = keep.tile([P, 1], F32, name="warm")
+        nc.vector.memset(warm[:], 0.0)
+        nc.scalar.activation(out=warm[:], in_=warm[:], func=GELU)
+
+        node_raw = keep.tile([P, FEAT], BF16, name="node_raw")
+        nc.sync.dma_start(out=node_raw[:], in_=node_rows)
+
+        weight_raw = []
+        for c in range(2 * PASSES):
+            raw = weights_in.tile([P, PACK, FEAT], BF16, name="weight_raw")
+            nc.sync.dma_start(
+                out=raw[:].rearrange("p (u e) m -> p u e m", u=2),
+                in_=W1_w[c * K_PASS : (c + 1) * K_PASS, :].rearrange("(u p e) m -> p u e m", u=2, e=2),
+            )
+            weight_raw.append(raw)
+
+        edge_raw = []
+
+        def load_edges(q):
+            raw = edges_in.tile([P, BLOCKS_PER_LOAD, FEAT], BF16, name="edge_raw")
+            nc.sync.dma_start(out=raw[:], in_=edge_rows[:, q * BLOCKS_PER_LOAD : (q + 1) * BLOCKS_PER_LOAD, :])
+            edge_raw.append(raw)
+
+        load_edges(0)
+        for h in range(PASSES):
+            raw = weights_in.tile([P, PACK, FEAT], BF16, name="weight_raw")
+            nc.sync.dma_start(
+                out=raw[:],
+                in_=W2_w[h * K_PASS : (h + 1) * K_PASS, :].rearrange("(j p) m -> p j m", p=P),
+            )
+            weight_raw.append(raw)
+        for q in range(1, BLOCKS // BLOCKS_PER_LOAD):
+            load_edges(q)
+
+        bias1_rows = keep.tile([P, P], BF16, name="bias1_rows")
+        nc.vector.memset(bias1_rows[:], 0.0)
+        nc.scalar.dma_start(out=bias1_rows[0 : FEAT // P, :], in_=W1_b.rearrange("(c p) -> c p", p=P))
+        bias2 = keep.tile([P, FEAT], BF16, name="bias2")
+        nc.scalar.dma_start(out=bias2[:], in_=W2_b.partition_broadcast(P))
+
+        def turn_features(x_bf16, grouped_bf16):
+            x_words = x_bf16.bitcast(F32)
+            turned = psum.tile([P, 2 * PASSES, P], F32, tag="bank", name="turned")
+            for w in range(2 * PASSES):
+                nc.tensor.transpose(turned[:, w, :], x_words[:, w * P : (w + 1) * P], ident[:])
+            nc.scalar.copy(
+                out=grouped_bf16.bitcast(F32).rearrange("p (g n u) -> p g n u", g=PASSES, u=2),
+                in_=turned[:].rearrange("p (g u) n -> p g n u", u=2),
+            )
+
+        node_grouped = keep.tile([P, FEAT], BF16, name="node_grouped", align_bytes=64)
+        node_codes = keep.tile([P, PASSES * P], U32, name="node_codes", align_bytes=64)
+        node_scales = keep.tile([P, PASSES * P], U8, name="node_scales", align_bytes=64)
+        turn_features(node_raw[:], node_grouped[:])
+        nc.vector.quantize_mx(out=node_codes[:].bitcast(FP8X4), scales=node_scales[:], in_=node_grouped[:])
+
+        bias1_rows_f32 = keep.tile([P, P], F32, name="bias1_rows_f32")
+        nc.vector.tensor_copy(out=bias1_rows_f32[:], in_=bias1_rows[:])
+        bias1_turned = psum.tile([P, P], F32, tag="bank", name="bias1_turned")
+        nc.tensor.transpose(bias1_turned[:], bias1_rows_f32[:], ident[:])
+        bias1 = keep.tile([P, FEAT // P], F32, name="bias1")
+        nc.vector.tensor_copy(out=bias1[:], in_=bias1_turned[:, 0 : FEAT // P])
+
+        weight_codes = keep.tile([P, 3 * PASSES, FEAT], U32, name="weight_codes", align_bytes=64)
+        weight_scales = keep.tile([P, 3 * PASSES, FEAT], U8, name="weight_scales", align_bytes=64)
+        weight_grouped = []
+
+        def regroup_weights(c):
+            grouped = regrouped.tile([P, FEAT, PACK], BF16, name="weight_grouped", align_bytes=64)
+            half = FEAT // 2
+            nc.vector.tensor_copy(
+                out=grouped[:, 0:half, :].rearrange("p (c i) t -> p c t i", i=4),
+                in_=weight_raw[c][:, :, 0:half].rearrange("p t (c i) -> p c t i", i=4),
+            )
+            nc.scalar.copy(
+                out=grouped[:, half:FEAT, :].rearrange("p (c i) t -> p c t i", i=4),
+                in_=weight_raw[c][:, :, half:FEAT].rearrange("p t (c i) -> p c t i", i=4),
+            )
+            weight_grouped.append(grouped)
+
+        def quantise_weights(c):
+            nc.vector.quantize_mx(
+                out=weight_codes[:, c, :].bitcast(FP8X4),
+                scales=weight_scales[:, c, :],
+                in_=weight_grouped[c][:].rearrange("p m t -> p (m t)"),
+            )
+
+        for c in range(3 * PASSES):
+            regroup_weights(c)
+            if c > 0:
+                quantise_weights(c - 1)
+        quantise_weights(3 * PASSES - 1)
+
+        def first_layer_product(first_pass, codes, scales, h):
+            acc = psum.tile([P, PACK, P], F32, tag="bank", name="acc1")
+            for j in range(PACK):
+                units = slice((h * PACK + j) * P, (h * PACK + j + 1) * P)
+                for g in range(PASSES):
+                    rows = slice(g * P, (g + 1) * P)
+                    nc.tensor.matmul_mx(
+                        out=acc[:, j, :],
+                        lhsT=weight_codes[:, first_pass + g, units].bitcast(FP8X4),
+                        lhsT_scale=weight_scales[:, first_pass + g, units],
+                        rhs=codes[:, rows].bitcast(FP8X4),
+                        rhs_scale=scales[:, rows],
+                        start=(g == 0),
+                        stop=(g == PASSES - 1),
+                    )
+            return acc
+
+        node_term = keep.tile([P, PASSES, P, PACK], F32, name="node_term")
+        for h in range(PASSES):
+            acc = first_layer_product(0, node_codes[:], node_scales[:], h)
+            nc.vector.tensor_tensor(
+                out=node_term[:, h, :, :],
+                in0=acc[:].rearrange("p j n -> p n j"),
+                in1=bias1[:, h * PACK : (h + 1) * PACK].unsqueeze(1).to_broadcast([P, P, PACK]),
+                op=ADD,
+            )
+
+        edge_codes = keep.tile([P, BLOCKS, PASSES * P], U32, name="edge_codes", align_bytes=64)
+        edge_scales = keep.tile([P, BLOCKS, PASSES * P], U8, name="edge_scales", align_bytes=64)
+        edge_grouped = {}
+        acc1 = {}
+        hidden = {}
+        hidden_codes = {}
+        hidden_scales = {}
+        acc2 = {}
+
+        def turn_edges(b):
+            grouped = stream.tile([P, TURN, FEAT], BF16, name="edge_grouped", align_bytes=64)
+            for i in range(TURN):
+                raw = edge_raw[(b + i) // BLOCKS_PER_LOAD]
+                turn_features(raw[:, (b + i) % BLOCKS_PER_LOAD, :], grouped[:, i, :])
+            edge_grouped[b] = grouped
+
+        def quantise_edges(b):
+            nc.vector.quantize_mx(
+                out=edge_codes[:, b : b + TURN, :].rearrange("p b w -> p (b w)").bitcast(FP8X4),
+                scales=edge_scales[:, b : b + TURN, :].rearrange("p b w -> p (b w)"),
+                in_=edge_grouped[b][:].rearrange("p b k -> p (b k)"),
+            )
+
+        def first_layer_matmuls(b):
+            acc1[b] = [
+                first_layer_product(PASSES, edge_codes[:, b, :], edge_scales[:, b, :], h) for h in range(PASSES)
+            ]
+
+        def first_layer_gelu(b):
+            pre = stream.tile([P, PASSES, P, PACK], F32, name="pre1")
+            hid = stream.tile([P, PASSES, P, PACK], BF16, name="hidden", align_bytes=64)
+            for h in range(PASSES):
+                nc.vector.tensor_tensor(
+                    out=pre[:, h, :, :],
+                    in0=acc1[b][h][:].rearrange("p j n -> p n j"),
+                    in1=node_term[:, h, :, :],
+                    op=ADD,
+                )
+                nc.scalar.activation(out=hid[:, h, :, :], in_=pre[:, h, :, :], func=GELU)
+            hidden[b] = hid
+
+        def quantise_hidden(b):
+            codes = stream.tile([P, PASSES * P], U32, name="hidden_codes", align_bytes=64)
+            scales = stream.tile([P, PASSES * P], U8, name="hidden_scales", align_bytes=64)
+            nc.vector.quantize_mx(
+                out=codes[:].bitcast(FP8X4), scales=scales[:], in_=hidden[b][:].rearrange("p h n j -> p (h n j)")
+            )
+            hidden_codes[b] = codes
+            hidden_scales[b] = scales
+
+        def second_layer_matmuls(b):
+            acc2[b] = []
+            for f in range(FEAT // BANK):
+                acc = psum.tile([P, BANK], F32, tag="bank", name="acc2")
+                for h in range(PASSES):
+                    nc.tensor.matmul_mx(
+                        out=acc[:],
+                        lhsT=hidden_codes[b][:, h * P : (h + 1) * P].bitcast(FP8X4),
+                        lhsT_scale=hidden_scales[b][:, h * P : (h + 1) * P],
+                        rhs=weight_codes[:, 2 * PASSES + h, f * BANK : (f + 1) * BANK].bitcast(FP8X4),
+                        rhs_scale=weight_scales[:, 2 * PASSES + h, f * BANK : (f + 1) * BANK],
+                        start=(h == 0),
+                        stop=(h == PASSES - 1),
+                    )
+                acc2[b].append(acc)
+
+        def second_layer_gelu_and_store(b):
+            pre = stream.tile([P, FEAT], F32, name="pre2")
+            result = stream.tile([P, FEAT], F32, name="result")
+            for f in range(FEAT // BANK):
+                units = slice(f * BANK, (f + 1) * BANK)
+                nc.vector.tensor_tensor(out=pre[:, units], in0=acc2[b][f][:], in1=bias2[:, units], op=ADD)
+                nc.scalar.activation(out=result[:, units], in_=pre[:, units], func=GELU)
+            nc.sync.dma_start(out=out_rows[:, b, :], in_=result[:])
+
+        for step in range(-LEAD, BLOCKS + 2):
+            turning = step + LEAD
+            if turning < BLOCKS and turning % TURN == 0:
+                turn_edges(turning)
+            if 0 <= step + 1 < BLOCKS:
+                first_layer_matmuls(step + 1)
+            if 0 <= step < BLOCKS:
+                first_layer_gelu(step)
+            if turning < BLOCKS and turning % TURN == 0:
+                quantise_edges(turning)
+            if 0 <= step - 1 < BLOCKS:
+                quantise_hidden(step - 1)
+                second_layer_matmuls(step - 1)
+            if 0 <= step - 2 < BLOCKS:
+                second_layer_gelu_and_store(step - 2)

@@ -17,10 +17,11 @@ K_PASS = P * PACK
 FEAT = 1024
 PASSES = FEAT // K_PASS
 BLOCKS = 16
-BLOCKS_PER_LOAD = 4
 BANK = 512
 TURN = 2
 LEAD = 3
+LAG = 3
+VECTOR_COLUMNS = 512
 
 FLOPS = 2 * (P * FEAT * FEAT + 2 * P * BLOCKS * FEAT * FEAT)
 
@@ -33,23 +34,31 @@ def tile_declayerj_pa_kernel(tc, h_V, h_E, W1_w, W1_b, W2_w, W2_b, out):
 
     with ExitStack() as ctx:
         keep = ctx.enter_context(tc.tile_pool(name="keep", bufs=1))
-        edges_in = ctx.enter_context(tc.tile_pool(name="edges_in", bufs=BLOCKS // BLOCKS_PER_LOAD))
+        edges_in = ctx.enter_context(tc.tile_pool(name="edges_in", bufs=BLOCKS // TURN))
         weights_in = ctx.enter_context(tc.tile_pool(name="weights_in", bufs=3 * PASSES))
         regrouped = ctx.enter_context(tc.tile_pool(name="regrouped", bufs=2))
         stream = ctx.enter_context(tc.tile_pool(name="stream", bufs=3))
+        waiting = ctx.enter_context(tc.tile_pool(name="waiting", bufs=LAG + 1))
         psum = ctx.enter_context(tc.psum_pool(name="psum", bufs=8))
 
         ident = keep.tile([P, P], F32, name="ident")
         make_identity(nc, ident[:])
+        ones = keep.tile([P, P], BF16, name="ones")
+        nc.vector.memset(ones[:], 1.0)
         warm = keep.tile([P, 1], F32, name="warm")
         nc.vector.memset(warm[:], 0.0)
         nc.scalar.activation(out=warm[:], in_=warm[:], func=GELU)
 
-        node_raw = keep.tile([P, FEAT], BF16, name="node_raw")
-        nc.sync.dma_start(out=node_raw[:], in_=node_rows)
+        bias1_rows = keep.tile([P, P], BF16, name="bias1_rows")
+        nc.vector.memset(bias1_rows[:], 0.0)
+        nc.sync.dma_start(out=bias1_rows[0 : FEAT // P, :], in_=W1_b.rearrange("(c p) -> c p", p=P))
+        bias2_row = keep.tile([P, FEAT], BF16, name="bias2_row")
+        nc.vector.memset(bias2_row[:], 0.0)
+        nc.sync.dma_start(out=bias2_row[0:1, :], in_=W2_b.rearrange("(o m) -> o m", o=1))
 
         weight_raw = []
-        for c in range(2 * PASSES):
+
+        def load_first_weights(c):
             raw = weights_in.tile([P, PACK, FEAT], BF16, name="weight_raw")
             nc.sync.dma_start(
                 out=raw[:].rearrange("p (u e) m -> p u e m", u=2),
@@ -57,29 +66,31 @@ def tile_declayerj_pa_kernel(tc, h_V, h_E, W1_w, W1_b, W2_w, W2_b, out):
             )
             weight_raw.append(raw)
 
-        edge_raw = []
-
-        def load_edges(q):
-            raw = edges_in.tile([P, BLOCKS_PER_LOAD, FEAT], BF16, name="edge_raw")
-            nc.sync.dma_start(out=raw[:], in_=edge_rows[:, q * BLOCKS_PER_LOAD : (q + 1) * BLOCKS_PER_LOAD, :])
-            edge_raw.append(raw)
-
-        load_edges(0)
-        for h in range(PASSES):
+        def load_second_weights(h):
             raw = weights_in.tile([P, PACK, FEAT], BF16, name="weight_raw")
             nc.sync.dma_start(
-                out=raw[:],
-                in_=W2_w[h * K_PASS : (h + 1) * K_PASS, :].rearrange("(j p) m -> p j m", p=P),
+                out=raw[:], in_=W2_w[h * K_PASS : (h + 1) * K_PASS, :].rearrange("(j p) m -> p j m", p=P)
             )
             weight_raw.append(raw)
-        for q in range(1, BLOCKS // BLOCKS_PER_LOAD):
-            load_edges(q)
 
-        bias1_rows = keep.tile([P, P], BF16, name="bias1_rows")
-        nc.vector.memset(bias1_rows[:], 0.0)
-        nc.scalar.dma_start(out=bias1_rows[0 : FEAT // P, :], in_=W1_b.rearrange("(c p) -> c p", p=P))
-        bias2 = keep.tile([P, FEAT], BF16, name="bias2")
-        nc.scalar.dma_start(out=bias2[:], in_=W2_b.partition_broadcast(P))
+        edge_raw = {}
+
+        def load_edges(b):
+            raw = edges_in.tile([P, TURN, FEAT], BF16, name="edge_raw")
+            nc.sync.dma_start(out=raw[:], in_=edge_rows[:, b : b + TURN, :])
+            edge_raw[b] = raw
+
+        node_raw = keep.tile([P, FEAT], BF16, name="node_raw")
+        load_first_weights(0)
+        load_edges(0)
+        nc.sync.dma_start(out=node_raw[:], in_=node_rows)
+        for c in range(1, 2 * PASSES):
+            load_first_weights(c)
+        load_edges(TURN)
+        for h in range(PASSES):
+            load_second_weights(h)
+        for b in range(2 * TURN, BLOCKS, TURN):
+            load_edges(b)
 
         def turn_features(x_bf16, grouped_bf16):
             x_words = x_bf16.bitcast(F32)
@@ -91,33 +102,19 @@ def tile_declayerj_pa_kernel(tc, h_V, h_E, W1_w, W1_b, W2_w, W2_b, out):
                 in_=turned[:].rearrange("p (g u) n -> p g n u", u=2),
             )
 
-        node_grouped = keep.tile([P, FEAT], BF16, name="node_grouped", align_bytes=64)
-        node_codes = keep.tile([P, PASSES * P], U32, name="node_codes", align_bytes=64)
-        node_scales = keep.tile([P, PASSES * P], U8, name="node_scales", align_bytes=64)
-        turn_features(node_raw[:], node_grouped[:])
-        nc.vector.quantize_mx(out=node_codes[:].bitcast(FP8X4), scales=node_scales[:], in_=node_grouped[:])
-
-        bias1_rows_f32 = keep.tile([P, P], F32, name="bias1_rows_f32")
-        nc.vector.tensor_copy(out=bias1_rows_f32[:], in_=bias1_rows[:])
-        bias1_turned = psum.tile([P, P], F32, tag="bank", name="bias1_turned")
-        nc.tensor.transpose(bias1_turned[:], bias1_rows_f32[:], ident[:])
-        bias1 = keep.tile([P, FEAT // P], F32, name="bias1")
-        nc.vector.tensor_copy(out=bias1[:], in_=bias1_turned[:, 0 : FEAT // P])
-
         weight_codes = keep.tile([P, 3 * PASSES, FEAT], U32, name="weight_codes", align_bytes=64)
         weight_scales = keep.tile([P, 3 * PASSES, FEAT], U8, name="weight_scales", align_bytes=64)
         weight_grouped = []
 
         def regroup_weights(c):
             grouped = regrouped.tile([P, FEAT, PACK], BF16, name="weight_grouped", align_bytes=64)
-            half = FEAT // 2
             nc.vector.tensor_copy(
-                out=grouped[:, 0:half, :].rearrange("p (c i) t -> p c t i", i=4),
-                in_=weight_raw[c][:, :, 0:half].rearrange("p t (c i) -> p c t i", i=4),
+                out=grouped[:, 0:VECTOR_COLUMNS, :].rearrange("p (c i) t -> p c t i", i=4),
+                in_=weight_raw[c][:, :, 0:VECTOR_COLUMNS].rearrange("p t (c i) -> p c t i", i=4),
             )
             nc.scalar.copy(
-                out=grouped[:, half:FEAT, :].rearrange("p (c i) t -> p c t i", i=4),
-                in_=weight_raw[c][:, :, half:FEAT].rearrange("p t (c i) -> p c t i", i=4),
+                out=grouped[:, VECTOR_COLUMNS:FEAT, :].rearrange("p (c i) t -> p c t i", i=4),
+                in_=weight_raw[c][:, :, VECTOR_COLUMNS:FEAT].rearrange("p t (c i) -> p c t i", i=4),
             )
             weight_grouped.append(grouped)
 
@@ -127,12 +124,6 @@ def tile_declayerj_pa_kernel(tc, h_V, h_E, W1_w, W1_b, W2_w, W2_b, out):
                 scales=weight_scales[:, c, :],
                 in_=weight_grouped[c][:].rearrange("p m t -> p (m t)"),
             )
-
-        for c in range(3 * PASSES):
-            regroup_weights(c)
-            if c > 0:
-                quantise_weights(c - 1)
-        quantise_weights(3 * PASSES - 1)
 
         def first_layer_product(first_pass, codes, scales, h):
             acc = psum.tile([P, PACK, P], F32, tag="bank", name="acc1")
@@ -151,16 +142,6 @@ def tile_declayerj_pa_kernel(tc, h_V, h_E, W1_w, W1_b, W2_w, W2_b, out):
                     )
             return acc
 
-        node_term = keep.tile([P, PASSES, P, PACK], F32, name="node_term")
-        for h in range(PASSES):
-            acc = first_layer_product(0, node_codes[:], node_scales[:], h)
-            nc.vector.tensor_tensor(
-                out=node_term[:, h, :, :],
-                in0=acc[:].rearrange("p j n -> p n j"),
-                in1=bias1[:, h * PACK : (h + 1) * PACK].unsqueeze(1).to_broadcast([P, P, PACK]),
-                op=ADD,
-            )
-
         edge_codes = keep.tile([P, BLOCKS, PASSES * P], U32, name="edge_codes", align_bytes=64)
         edge_scales = keep.tile([P, BLOCKS, PASSES * P], U8, name="edge_scales", align_bytes=64)
         edge_grouped = {}
@@ -173,8 +154,7 @@ def tile_declayerj_pa_kernel(tc, h_V, h_E, W1_w, W1_b, W2_w, W2_b, out):
         def turn_edges(b):
             grouped = stream.tile([P, TURN, FEAT], BF16, name="edge_grouped", align_bytes=64)
             for i in range(TURN):
-                raw = edge_raw[(b + i) // BLOCKS_PER_LOAD]
-                turn_features(raw[:, (b + i) % BLOCKS_PER_LOAD, :], grouped[:, i, :])
+                turn_features(edge_raw[b][:, i, :], grouped[:, i, :])
             edge_grouped[b] = grouped
 
         def quantise_edges(b):
@@ -203,8 +183,8 @@ def tile_declayerj_pa_kernel(tc, h_V, h_E, W1_w, W1_b, W2_w, W2_b, out):
             hidden[b] = hid
 
         def quantise_hidden(b):
-            codes = stream.tile([P, PASSES * P], U32, name="hidden_codes", align_bytes=64)
-            scales = stream.tile([P, PASSES * P], U8, name="hidden_scales", align_bytes=64)
+            codes = waiting.tile([P, PASSES * P], U32, name="hidden_codes", align_bytes=64)
+            scales = waiting.tile([P, PASSES * P], U8, name="hidden_scales", align_bytes=64)
             nc.vector.quantize_mx(
                 out=codes[:].bitcast(FP8X4), scales=scales[:], in_=hidden[b][:].rearrange("p h n j -> p (h n j)")
             )
@@ -236,18 +216,67 @@ def tile_declayerj_pa_kernel(tc, h_V, h_E, W1_w, W1_b, W2_w, W2_b, out):
                 nc.scalar.activation(out=result[:, units], in_=pre[:, units], func=GELU)
             nc.sync.dma_start(out=out_rows[:, b, :], in_=result[:])
 
-        for step in range(-LEAD, BLOCKS + 2):
+        regroup_weights(0)
+        turn_edges(0)
+
+        node_grouped = keep.tile([P, FEAT], BF16, name="node_grouped", align_bytes=64)
+        node_codes = keep.tile([P, PASSES * P], U32, name="node_codes", align_bytes=64)
+        node_scales = keep.tile([P, PASSES * P], U8, name="node_scales", align_bytes=64)
+        turn_features(node_raw[:], node_grouped[:])
+
+        bias1_rows_f32 = keep.tile([P, P], F32, name="bias1_rows_f32")
+        nc.vector.tensor_copy(out=bias1_rows_f32[:], in_=bias1_rows[:])
+        bias1_turned = psum.tile([P, P], F32, tag="bank", name="bias1_turned")
+        nc.tensor.transpose(bias1_turned[:], bias1_rows_f32[:], ident[:])
+        bias1 = keep.tile([P, FEAT // P], F32, name="bias1")
+        nc.vector.tensor_copy(out=bias1[:], in_=bias1_turned[:, 0 : FEAT // P])
+
+        bias2 = keep.tile([P, FEAT], F32, name="bias2")
+        for f in range(FEAT // BANK):
+            units = slice(f * BANK, (f + 1) * BANK)
+            spread = psum.tile([P, BANK], F32, tag="bank", name="spread")
+            nc.tensor.matmul(out=spread[:], lhsT=ones[:], rhs=bias2_row[:, units], start=True, stop=True)
+            nc.scalar.copy(out=bias2[:, units], in_=spread[:])
+
+        quantise_edges(0)
+        nc.vector.quantize_mx(out=node_codes[:].bitcast(FP8X4), scales=node_scales[:], in_=node_grouped[:])
+
+        for c in range(1, 2 * PASSES):
+            regroup_weights(c)
+            quantise_weights(c - 1)
+        quantise_weights(2 * PASSES - 1)
+
+        node_term = keep.tile([P, PASSES, P, PACK], F32, name="node_term")
+        for h in range(PASSES):
+            acc = first_layer_product(0, node_codes[:], node_scales[:], h)
+            nc.vector.tensor_tensor(
+                out=node_term[:, h, :, :],
+                in0=acc[:].rearrange("p j n -> p n j"),
+                in1=bias1[:, h * PACK : (h + 1) * PACK].unsqueeze(1).to_broadcast([P, P, PACK]),
+                op=ADD,
+            )
+
+        def live(b):
+            return 0 <= b < BLOCKS
+
+        for step in range(-1, BLOCKS + LAG + 1):
             turning = step + LEAD
-            if turning < BLOCKS and turning % TURN == 0:
+            turns = TURN <= turning < BLOCKS and turning % TURN == 0
+            if turns:
                 turn_edges(turning)
-            if 0 <= step + 1 < BLOCKS:
+            if live(step + 1):
                 first_layer_matmuls(step + 1)
-            if 0 <= step < BLOCKS:
+            if live(step):
                 first_layer_gelu(step)
-            if turning < BLOCKS and turning % TURN == 0:
+            if turns:
                 quantise_edges(turning)
-            if 0 <= step - 1 < BLOCKS:
+            if 0 <= step < PASSES:
+                regroup_weights(2 * PASSES + step)
+            if 1 <= step <= PASSES:
+                quantise_weights(2 * PASSES + step - 1)
+            if live(step - 1):
                 quantise_hidden(step - 1)
-                second_layer_matmuls(step - 1)
-            if 0 <= step - 2 < BLOCKS:
-                second_layer_gelu_and_store(step - 2)
+            if live(step - LAG):
+                second_layer_matmuls(step - LAG)
+            if live(step - LAG - 1):
+                second_layer_gelu_and_store(step - LAG - 1)

@@ -21,7 +21,7 @@ BANK = 512
 TURN = 2
 LEAD = 3
 LAG = 3
-VECTOR_COLUMNS = 512
+VECTOR_COLUMNS = 256
 
 FLOPS = 2 * (P * FEAT * FEAT + 2 * P * BLOCKS * FEAT * FEAT)
 

@@ -21,6 +21,7 @@ BANK = 512
 TURN = 2
 LEAD = 3
 LAG = 3
+PIECE = 512
 VECTOR_COLUMNS = 256
 
 FLOPS = 2 * (P * FEAT * FEAT + 2 * P * BLOCKS * FEAT * FEAT)
@@ -36,7 +37,7 @@ def tile_declayerj_pa_kernel(tc, h_V, h_E, W1_w, W1_b, W2_w, W2_b, out):
         keep = ctx.enter_context(tc.tile_pool(name="keep", bufs=1))
         edges_in = ctx.enter_context(tc.tile_pool(name="edges_in", bufs=BLOCKS // TURN))
         weights_in = ctx.enter_context(tc.tile_pool(name="weights_in", bufs=3 * PASSES))
-        regrouped = ctx.enter_context(tc.tile_pool(name="regrouped", bufs=2))
+        regrouped = ctx.enter_context(tc.tile_pool(name="regrouped", bufs=4))
         stream = ctx.enter_context(tc.tile_pool(name="stream", bufs=3))
         waiting = ctx.enter_context(tc.tile_pool(name="waiting", bufs=LAG + 1))
         psum = ctx.enter_context(tc.psum_pool(name="psum", bufs=8))
@@ -104,26 +105,30 @@ def tile_declayerj_pa_kernel(tc, h_V, h_E, W1_w, W1_b, W2_w, W2_b, out):
 
         weight_codes = keep.tile([P, 3 * PASSES, FEAT], U32, name="weight_codes", align_bytes=64)
         weight_scales = keep.tile([P, 3 * PASSES, FEAT], U8, name="weight_scales", align_bytes=64)
-        weight_grouped = []
+        weight_grouped = {}
 
         def regroup_weights(c):
-            grouped = regrouped.tile([P, FEAT, PACK], BF16, name="weight_grouped", align_bytes=64)
-            nc.vector.tensor_copy(
-                out=grouped[:, 0:VECTOR_COLUMNS, :].rearrange("p (c i) t -> p c t i", i=4),
-                in_=weight_raw[c][:, :, 0:VECTOR_COLUMNS].rearrange("p t (c i) -> p c t i", i=4),
-            )
-            nc.scalar.copy(
-                out=grouped[:, VECTOR_COLUMNS:FEAT, :].rearrange("p (c i) t -> p c t i", i=4),
-                in_=weight_raw[c][:, :, VECTOR_COLUMNS:FEAT].rearrange("p t (c i) -> p c t i", i=4),
-            )
-            weight_grouped.append(grouped)
+            for piece in range(FEAT // PIECE):
+                grouped = regrouped.tile([P, PIECE, PACK], BF16, name="weight_grouped", align_bytes=64)
+                raw = weight_raw[c][:, :, piece * PIECE : (piece + 1) * PIECE]
+                nc.vector.tensor_copy(
+                    out=grouped[:, 0:VECTOR_COLUMNS, :].rearrange("p (c i) t -> p c t i", i=4),
+                    in_=raw[:, :, 0:VECTOR_COLUMNS].rearrange("p t (c i) -> p c t i", i=4),
+                )
+                nc.scalar.copy(
+                    out=grouped[:, VECTOR_COLUMNS:PIECE, :].rearrange("p (c i) t -> p c t i", i=4),
+                    in_=raw[:, :, VECTOR_COLUMNS:PIECE].rearrange("p t (c i) -> p c t i", i=4),
+                )
+                weight_grouped[(c, piece)] = grouped
 
         def quantise_weights(c):
-            nc.vector.quantize_mx(
-                out=weight_codes[:, c, :].bitcast(FP8X4),
-                scales=weight_scales[:, c, :],
-                in_=weight_grouped[c][:].rearrange("p m t -> p (m t)"),
-            )
+            for piece in range(FEAT // PIECE):
+                columns = slice(piece * PIECE, (piece + 1) * PIECE)
+                nc.vector.quantize_mx(
+                    out=weight_codes[:, c, columns].bitcast(FP8X4),
+                    scales=weight_scales[:, c, columns],
+                    in_=weight_grouped[(c, piece)][:].rearrange("p m t -> p (m t)"),
+                )
 
         def first_layer_product(first_pass, codes, scales, h):
             acc = psum.tile([P, PACK, P], F32, tag="bank", name="acc1")
@@ -214,7 +219,7 @@ def tile_declayerj_pa_kernel(tc, h_V, h_E, W1_w, W1_b, W2_w, W2_b, out):
                 units = slice(f * BANK, (f + 1) * BANK)
                 nc.vector.tensor_tensor(out=pre[:, units], in0=acc2[b][f][:], in1=bias2[:, units], op=ADD)
                 nc.scalar.activation(out=result[:, units], in_=pre[:, units], func=GELU)
-            nc.sync.dma_start(out=out_rows[:, b, :], in_=result[:])
+                nc.sync.dma_start(out=out_rows[:, b, units], in_=result[:, units])
 
         regroup_weights(0)
         turn_edges(0)

@@ -39,7 +39,7 @@ def tile_declayerj_pa_kernel(tc, h_V, h_E, W1_w, W1_b, W2_w, W2_b, out):
         weights_in = ctx.enter_context(tc.tile_pool(name="weights_in", bufs=3 * PASSES))
         regrouped = ctx.enter_context(tc.tile_pool(name="regrouped", bufs=4))
         stream = ctx.enter_context(tc.tile_pool(name="stream", bufs=3))
-        waiting = ctx.enter_context(tc.tile_pool(name="waiting", bufs=LAG + 1))
+        waiting = ctx.enter_context(tc.tile_pool(name="waiting", bufs=LAG + 2))
         psum = ctx.enter_context(tc.psum_pool(name="psum", bufs=8))
 
         ident = keep.tile([P, P], F32, name="ident")
@@ -93,13 +93,13 @@ def tile_declayerj_pa_kernel(tc, h_V, h_E, W1_w, W1_b, W2_w, W2_b, out):
         for b in range(2 * TURN, BLOCKS, TURN):
             load_edges(b)
 
-        def turn_features(x_bf16, grouped_bf16):
+        def turn_features(x_bf16, grouped_words):
             x_words = x_bf16.bitcast(F32)
             turned = psum.tile([P, 2 * PASSES, P], F32, tag="bank", name="turned")
             for w in range(2 * PASSES):
                 nc.tensor.transpose(turned[:, w, :], x_words[:, w * P : (w + 1) * P], ident[:])
             nc.scalar.copy(
-                out=grouped_bf16.bitcast(F32).rearrange("p (g n u) -> p g n u", g=PASSES, u=2),
+                out=grouped_words,
                 in_=turned[:].rearrange("p (g u) n -> p g n u", u=2),
             )
 
@@ -130,12 +130,13 @@ def tile_declayerj_pa_kernel(tc, h_V, h_E, W1_w, W1_b, W2_w, W2_b, out):
                     in_=weight_grouped[(c, piece)][:].rearrange("p m t -> p (m t)"),
                 )
 
-        def first_layer_product(first_pass, codes, scales, h):
-            acc = psum.tile([P, PACK, P], F32, tag="bank", name="acc1")
-            for j in range(PACK):
-                units = slice((h * PACK + j) * P, (h * PACK + j + 1) * P)
+        def first_layer_product(first_pass, codes, scales, first_unit, width):
+            groups = BANK // width
+            acc = psum.tile([P, groups, width], F32, tag="bank", name="acc1")
+            for j in range(groups):
+                units = slice(first_unit + j * P, first_unit + (j + 1) * P)
                 for g in range(PASSES):
-                    rows = slice(g * P, (g + 1) * P)
+                    rows = slice(g * width, (g + 1) * width)
                     nc.tensor.matmul_mx(
                         out=acc[:, j, :],
                         lhsT=weight_codes[:, first_pass + g, units].bitcast(FP8X4),
@@ -147,8 +148,8 @@ def tile_declayerj_pa_kernel(tc, h_V, h_E, W1_w, W1_b, W2_w, W2_b, out):
                     )
             return acc
 
-        edge_codes = keep.tile([P, BLOCKS, PASSES * P], U32, name="edge_codes", align_bytes=64)
-        edge_scales = keep.tile([P, BLOCKS, PASSES * P], U8, name="edge_scales", align_bytes=64)
+        edge_codes = keep.tile([P, BLOCKS // TURN, PASSES * TURN * P], U32, name="edge_codes", align_bytes=64)
+        edge_scales = keep.tile([P, BLOCKS // TURN, PASSES * TURN * P], U8, name="edge_scales", align_bytes=64)
         edge_grouped = {}
         acc1 = {}
         hidden = {}
@@ -157,54 +158,66 @@ def tile_declayerj_pa_kernel(tc, h_V, h_E, W1_w, W1_b, W2_w, W2_b, out):
         acc2 = {}
 
         def turn_edges(b):
-            grouped = stream.tile([P, TURN, FEAT], BF16, name="edge_grouped", align_bytes=64)
+            grouped = stream.tile([P, TURN * FEAT], BF16, name="edge_grouped", align_bytes=64)
+            words = grouped[:].bitcast(F32).rearrange("p (g b n u) -> p g b n u", g=PASSES, b=TURN, u=2)
             for i in range(TURN):
-                turn_features(edge_raw[b][:, i, :], grouped[:, i, :])
+                turn_features(edge_raw[b][:, i, :], words[:, :, i, :, :])
             edge_grouped[b] = grouped
 
         def quantise_edges(b):
             nc.vector.quantize_mx(
-                out=edge_codes[:, b : b + TURN, :].rearrange("p b w -> p (b w)").bitcast(FP8X4),
-                scales=edge_scales[:, b : b + TURN, :].rearrange("p b w -> p (b w)"),
-                in_=edge_grouped[b][:].rearrange("p b k -> p (b k)"),
+                out=edge_codes[:, b // TURN, :].bitcast(FP8X4),
+                scales=edge_scales[:, b // TURN, :],
+                in_=edge_grouped[b][:],
             )
 
-        def first_layer_matmuls(b):
-            acc1[b] = [
-                first_layer_product(PASSES, edge_codes[:, b, :], edge_scales[:, b, :], h) for h in range(PASSES)
+        def first_layer_matmuls(k):
+            pair, h = divmod(k, 2)
+            acc1[k] = [
+                first_layer_product(
+                    PASSES, edge_codes[:, pair, :], edge_scales[:, pair, :], h * K_PASS + q * 2 * P, TURN * P
+                )
+                for q in range(2)
             ]
 
-        def first_layer_gelu(b):
-            pre = stream.tile([P, PASSES, P, PACK], F32, name="pre1")
-            hid = stream.tile([P, PASSES, P, PACK], BF16, name="hidden", align_bytes=64)
-            for h in range(PASSES):
+        def first_layer_gelu(k):
+            h = k % 2
+            pre = stream.tile([P, 2, TURN, P, 2], F32, name="pre1")
+            hid = stream.tile([P, TURN * P, PACK], BF16, name="hidden", align_bytes=64)
+            for q in range(2):
                 nc.vector.tensor_tensor(
-                    out=pre[:, h, :, :],
-                    in0=acc1[b][h][:].rearrange("p j n -> p n j"),
-                    in1=node_term[:, h, :, :],
+                    out=pre[:, q, :, :, :],
+                    in0=acc1[k][q][:].rearrange("p j (b n) -> p b n j", b=TURN),
+                    in1=node_term[:, h, q, :, :].unsqueeze(1).to_broadcast([P, TURN, P, 2]),
                     op=ADD,
                 )
-                nc.scalar.activation(out=hid[:, h, :, :], in_=pre[:, h, :, :], func=GELU)
-            hidden[b] = hid
-
-        def quantise_hidden(b):
-            codes = waiting.tile([P, PASSES * P], U32, name="hidden_codes", align_bytes=64)
-            scales = waiting.tile([P, PASSES * P], U8, name="hidden_scales", align_bytes=64)
-            nc.vector.quantize_mx(
-                out=codes[:].bitcast(FP8X4), scales=scales[:], in_=hidden[b][:].rearrange("p h n j -> p (h n j)")
+            nc.scalar.activation(
+                out=hid[:].rearrange("p r (q j) -> p r q j", q=2),
+                in_=pre[:].rearrange("p q b n j -> p (b n) q j"),
+                func=GELU,
             )
-            hidden_codes[b] = codes
-            hidden_scales[b] = scales
+            hidden[k] = hid
+
+        def quantise_hidden(k):
+            codes = waiting.tile([P, TURN * P], U32, name="hidden_codes", align_bytes=64)
+            scales = waiting.tile([P, TURN * P], U8, name="hidden_scales", align_bytes=64)
+            nc.vector.quantize_mx(
+                out=codes[:].bitcast(FP8X4), scales=scales[:], in_=hidden[k][:].rearrange("p r j -> p (r j)")
+            )
+            hidden_codes[k] = codes
+            hidden_scales[k] = scales
 
         def second_layer_matmuls(b):
             acc2[b] = []
+            pair, i = divmod(b, TURN)
+            rows = slice(i * P, (i + 1) * P)
             for f in range(FEAT // BANK):
                 acc = psum.tile([P, BANK], F32, tag="bank", name="acc2")
                 for h in range(PASSES):
                     nc.tensor.matmul_mx(
                         out=acc[:],
-                        lhsT=hidden_codes[b][:, h * P : (h + 1) * P].bitcast(FP8X4),
-                        lhsT_scale=hidden_scales[b][:, h * P : (h + 1) * P],
+                        lhsT=hidden_codes[2 * pair + h][:, rows].bitcast(FP8X4),
+                        lhsT_scale=hidden_scales[2 * pair + h][:, rows],
                         rhs=weight_codes[:, 2 * PASSES + h, f * BANK : (f + 1) * BANK].bitcast(FP8X4),
                         rhs_scale=weight_scales[:, 2 * PASSES + h, f * BANK : (f + 1) * BANK],
                         start=(h == 0),
@@ -227,7 +240,9 @@ def tile_declayerj_pa_kernel(tc, h_V, h_E, W1_w, W1_b, W2_w, W2_b, out):
         node_grouped = keep.tile([P, FEAT], BF16, name="node_grouped", align_bytes=64)
         node_codes = keep.tile([P, PASSES * P], U32, name="node_codes", align_bytes=64)
         node_scales = keep.tile([P, PASSES * P], U8, name="node_scales", align_bytes=64)
-        turn_features(node_raw[:], node_grouped[:])
+        turn_features(
+            node_raw[:], node_grouped[:].bitcast(F32).rearrange("p (g n u) -> p g n u", g=PASSES, u=2)
+        )
 
         bias1_rows_f32 = keep.tile([P, P], F32, name="bias1_rows_f32")
         nc.vector.tensor_copy(out=bias1_rows_f32[:], in_=bias1_rows[:])
@@ -251,13 +266,14 @@ def tile_declayerj_pa_kernel(tc, h_V, h_E, W1_w, W1_b, W2_w, W2_b, out):
             quantise_weights(c - 1)
         quantise_weights(2 * PASSES - 1)
 
-        node_term = keep.tile([P, PASSES, P, PACK], F32, name="node_term")
+        node_term = keep.tile([P, PASSES, 2, P, 2], F32, name="node_term")
         for h in range(PASSES):
-            acc = first_layer_product(0, node_codes[:], node_scales[:], h)
+            acc = first_layer_product(0, node_codes[:], node_scales[:], h * K_PASS, P)
+            bias = bias1[:, h * PACK : (h + 1) * PACK].rearrange("p (q j) -> p q j", q=2)
             nc.vector.tensor_tensor(
-                out=node_term[:, h, :, :],
-                in0=acc[:].rearrange("p j n -> p n j"),
-                in1=bias1[:, h * PACK : (h + 1) * PACK].unsqueeze(1).to_broadcast([P, P, PACK]),
+                out=node_term[:, h, :, :, :],
+                in0=acc[:].rearrange("p (q j) n -> p q n j", q=2),
+                in1=bias.unsqueeze(2).to_broadcast([P, 2, P, 2]),
                 op=ADD,
             )
 

@@ -36,7 +36,8 @@ def tile_declayerj_pa_kernel(tc, h_V, h_E, W1_w, W1_b, W2_w, W2_b, out):
     with ExitStack() as ctx:
         keep = ctx.enter_context(tc.tile_pool(name="keep", bufs=1))
         edges_in = ctx.enter_context(tc.tile_pool(name="edges_in", bufs=BLOCKS // TURN))
-        weights_in = ctx.enter_context(tc.tile_pool(name="weights_in", bufs=3 * PASSES))
+        weights_in = ctx.enter_context(tc.tile_pool(name="weights_in", bufs=3 * PASSES - 1))
+        first_in = ctx.enter_context(tc.tile_pool(name="first_in", bufs=FEAT // PIECE))
         regrouped = ctx.enter_context(tc.tile_pool(name="regrouped", bufs=4))
         stream = ctx.enter_context(tc.tile_pool(name="stream", bufs=3))
         waiting = ctx.enter_context(tc.tile_pool(name="waiting", bufs=LAG + 2))
@@ -52,10 +53,8 @@ def tile_declayerj_pa_kernel(tc, h_V, h_E, W1_w, W1_b, W2_w, W2_b, out):
 
         bias1_rows = keep.tile([P, P], BF16, name="bias1_rows")
         nc.vector.memset(bias1_rows[:], 0.0)
-        nc.sync.dma_start(out=bias1_rows[0 : FEAT // P, :], in_=W1_b.rearrange("(c p) -> c p", p=P))
         bias2_row = keep.tile([P, FEAT], BF16, name="bias2_row")
         nc.vector.memset(bias2_row[:], 0.0)
-        nc.sync.dma_start(out=bias2_row[0:1, :], in_=W2_b.rearrange("(o m) -> o m", o=1))
 
         weight_raw = []
 
@@ -65,14 +64,26 @@ def tile_declayerj_pa_kernel(tc, h_V, h_E, W1_w, W1_b, W2_w, W2_b, out):
                 out=raw[:].rearrange("p (u e) m -> p u e m", u=2),
                 in_=W1_w[c * K_PASS : (c + 1) * K_PASS, :].rearrange("(u p e) m -> p u e m", u=2, e=2),
             )
-            weight_raw.append(raw)
+            weight_raw.append([raw[:, :, m : m + PIECE] for m in range(0, FEAT, PIECE)])
+
+        def load_first_weights_in_pieces(c):
+            pieces = []
+            for m in range(0, FEAT, PIECE):
+                raw = first_in.tile([P, PACK, PIECE], BF16, name="first_raw")
+                for u in range(2):
+                    rows = W1_w[c * K_PASS + u * 2 * P : c * K_PASS + (u + 1) * 2 * P, m : m + PIECE]
+                    nc.sync.dma_start(
+                        out=raw[:, 2 * u : 2 * u + 2, :], in_=rows.rearrange("(p e) m -> p e m", e=2)
+                    )
+                pieces.append(raw[:])
+            weight_raw.append(pieces)
 
         def load_second_weights(h):
             raw = weights_in.tile([P, PACK, FEAT], BF16, name="weight_raw")
             nc.sync.dma_start(
                 out=raw[:], in_=W2_w[h * K_PASS : (h + 1) * K_PASS, :].rearrange("(j p) m -> p j m", p=P)
             )
-            weight_raw.append(raw)
+            weight_raw.append([raw[:, :, m : m + PIECE] for m in range(0, FEAT, PIECE)])
 
         edge_raw = {}
 
@@ -82,11 +93,14 @@ def tile_declayerj_pa_kernel(tc, h_V, h_E, W1_w, W1_b, W2_w, W2_b, out):
             edge_raw[b] = raw
 
         node_raw = keep.tile([P, FEAT], BF16, name="node_raw")
-        load_first_weights(0)
+        load_first_weights_in_pieces(0)
+        load_first_weights(1)
         load_edges(0)
+        nc.sync.dma_start(out=bias1_rows[0 : FEAT // P, :], in_=W1_b.rearrange("(c p) -> c p", p=P))
+        load_first_weights(2)
         nc.sync.dma_start(out=node_raw[:], in_=node_rows)
-        for c in range(1, 2 * PASSES):
-            load_first_weights(c)
+        load_first_weights(3)
+        nc.sync.dma_start(out=bias2_row[0:1, :], in_=W2_b.rearrange("(o m) -> o m", o=1))
         load_edges(TURN)
         for h in range(PASSES):
             load_second_weights(h)
@@ -110,7 +124,7 @@ def tile_declayerj_pa_kernel(tc, h_V, h_E, W1_w, W1_b, W2_w, W2_b, out):
         def regroup_weights(c):
             for piece in range(FEAT // PIECE):
                 grouped = regrouped.tile([P, PIECE, PACK], BF16, name="weight_grouped", align_bytes=64)
-                raw = weight_raw[c][:, :, piece * PIECE : (piece + 1) * PIECE]
+                raw = weight_raw[c][piece]
                 nc.vector.tensor_copy(
                     out=grouped[:, 0:VECTOR_COLUMNS, :].rearrange("p (c i) t -> p c t i", i=4),
                     in_=raw[:, :, 0:VECTOR_COLUMNS].rearrange("p t (c i) -> p c t i", i=4),
@@ -228,9 +242,13 @@ def tile_declayerj_pa_kernel(tc, h_V, h_E, W1_w, W1_b, W2_w, W2_b, out):
         def second_layer_gelu_and_store(b):
             pre = stream.tile([P, FEAT], F32, name="pre2")
             result = stream.tile([P, FEAT], F32, name="result")
-            for f in range(FEAT // BANK):
-                units = slice(f * BANK, (f + 1) * BANK)
-                nc.vector.tensor_tensor(out=pre[:, units], in0=acc2[b][f][:], in1=bias2[:, units], op=ADD)
+            width = BANK // 2 if b == BLOCKS - 1 else BANK
+            for m in range(0, FEAT, width):
+                f, start = divmod(m, BANK)
+                units = slice(m, m + width)
+                nc.vector.tensor_tensor(
+                    out=pre[:, units], in0=acc2[b][f][:, start : start + width], in1=bias2[:, units], op=ADD
+                )
                 nc.scalar.activation(out=result[:, units], in_=pre[:, units], func=GELU)
                 nc.sync.dma_start(out=out_rows[:, b, units], in_=result[:, units])
 

from contextlib import ExitStack

import concourse.mybir as mybir
from concourse.masks import make_identity

F32 = mybir.dt.float32
BF16 = mybir.dt.bfloat16
U32 = mybir.dt.uint32
U8 = mybir.dt.uint8
FP8X4 = mybir.dt.float8_e4m3fn_x4
GELU = mybir.ActivationFunctionType.Gelu_apprx_tanh
ADD = mybir.AluOpType.add

P = 128
PACK = 4
K_PASS = P * PACK
FEAT = 1024
PASSES = FEAT // K_PASS
BLOCKS = 16
BANK = 512
TURN = 2
LEAD = 3
LAG = 3
PIECE = 512
VECTOR_COLUMNS = 256

FLOPS = 2 * (P * FEAT * FEAT + 2 * P * BLOCKS * FEAT * FEAT)


def tile_declayerj_pa_kernel(tc, h_V, h_E, W1_w, W1_b, W2_w, W2_b, out):
    nc = tc.nc
    node_rows = h_V.rearrange("b n c -> (b n) c")
    edge_rows = h_E.rearrange("b n k c -> (b n) k c")
    out_rows = out.rearrange("b n k m -> (b n) k m")

    with ExitStack() as ctx:
        keep = ctx.enter_context(tc.tile_pool(name="keep", bufs=1))
        edges_in = ctx.enter_context(tc.tile_pool(name="edges_in", bufs=BLOCKS // TURN))
        weights_in = ctx.enter_context(tc.tile_pool(name="weights_in", bufs=3 * PASSES - 1))
        first_in = ctx.enter_context(tc.tile_pool(name="first_in", bufs=FEAT // PIECE))
        regrouped = ctx.enter_context(tc.tile_pool(name="regrouped", bufs=4))
        stream = ctx.enter_context(tc.tile_pool(name="stream", bufs=3))
        waiting = ctx.enter_context(tc.tile_pool(name="waiting", bufs=LAG + 2))
        psum = ctx.enter_context(tc.psum_pool(name="psum", bufs=8))

        ident = keep.tile([P, P], F32, name="ident")
        make_identity(nc, ident[:])
        ones = keep.tile([P, P], BF16, name="ones")
        nc.vector.memset(ones[:], 1.0)
        warm = keep.tile([P, 1], F32, name="warm")
        nc.vector.memset(warm[:], 0.0)
        nc.scalar.activation(out=warm[:], in_=warm[:], func=GELU)

        bias1_rows = keep.tile([P, P], BF16, name="bias1_rows")
        nc.vector.memset(bias1_rows[:], 0.0)
        bias2_row = keep.tile([P, FEAT], BF16, name="bias2_row")
        nc.vector.memset(bias2_row[:], 0.0)

        weight_raw = []

        def load_first_weights(c):
            raw = weights_in.tile([P, PACK, FEAT], BF16, name="weight_raw")
            nc.sync.dma_start(
                out=raw[:].rearrange("p (u e) m -> p u e m", u=2),
                in_=W1_w[c * K_PASS : (c + 1) * K_PASS, :].rearrange("(u p e) m -> p u e m", u=2, e=2),
            )
            weight_raw.append([raw[:, :, m : m + PIECE] for m in range(0, FEAT, PIECE)])

        def load_first_weights_in_pieces(c):
            pieces = []
            for m in range(0, FEAT, PIECE):
                raw = first_in.tile([P, PACK, PIECE], BF16, name="first_raw")
                for u in range(2):
                    rows = W1_w[c * K_PASS + u * 2 * P : c * K_PASS + (u + 1) * 2 * P, m : m + PIECE]
                    nc.sync.dma_start(
                        out=raw[:, 2 * u : 2 * u + 2, :], in_=rows.rearrange("(p e) m -> p e m", e=2)
                    )
                pieces.append(raw[:])
            weight_raw.append(pieces)

        def load_second_weights(h):
            raw = weights_in.tile([P, PACK, FEAT], BF16, name="weight_raw")
            nc.sync.dma_start(
                out=raw[:], in_=W2_w[h * K_PASS : (h + 1) * K_PASS, :].rearrange("(j p) m -> p j m", p=P)
            )
            weight_raw.append([raw[:, :, m : m + PIECE] for m in range(0, FEAT, PIECE)])

        edge_raw = {}

        def load_edges(b):
            raw = edges_in.tile([P, TURN, FEAT], BF16, name="edge_raw")
            nc.sync.dma_start(out=raw[:], in_=edge_rows[:, b : b + TURN, :])
            edge_raw[b] = raw

        node_raw = keep.tile([P, FEAT], BF16, name="node_raw")
        load_first_weights_in_pieces(0)
        load_first_weights(1)
        load_edges(0)
        nc.sync.dma_start(out=bias1_rows[0 : FEAT // P, :], in_=W1_b.rearrange("(c p) -> c p", p=P))
        load_first_weights(2)
        nc.sync.dma_start(out=node_raw[:], in_=node_rows)
        load_first_weights(3)
        nc.sync.dma_start(out=bias2_row[0:1, :], in_=W2_b.rearrange("(o m) -> o m", o=1))
        load_edges(TURN)
        for h in range(PASSES):
            load_second_weights(h)
        for b in range(2 * TURN, BLOCKS, TURN):
            load_edges(b)

        def turn_features(x_bf16, grouped_words):
            x_words = x_bf16.bitcast(F32)
            turned = psum.tile([P, 2 * PASSES, P], F32, tag="bank", name="turned")
            for w in range(2 * PASSES):
                nc.tensor.transpose(turned[:, w, :], x_words[:, w * P : (w + 1) * P], ident[:])
            nc.scalar.copy(
                out=grouped_words,
                in_=turned[:].rearrange("p (g u) n -> p g n u", u=2),
            )

        weight_codes = keep.tile([P, 3 * PASSES, FEAT], U32, name="weight_codes", align_bytes=64)
        weight_scales = keep.tile([P, 3 * PASSES, FEAT], U8, name="weight_scales", align_bytes=64)
        weight_grouped = {}

        def regroup_weights(c):
            for piece in range(FEAT // PIECE):
                grouped = regrouped.tile([P, PIECE, PACK], BF16, name="weight_grouped", align_bytes=64)
                raw = weight_raw[c][piece]
                nc.vector.tensor_copy(
                    out=grouped[:, 0:VECTOR_COLUMNS, :].rearrange("p (c i) t -> p c t i", i=4),
                    in_=raw[:, :, 0:VECTOR_COLUMNS].rearrange("p t (c i) -> p c t i", i=4),
                )
                nc.scalar.copy(
                    out=grouped[:, VECTOR_COLUMNS:PIECE, :].rearrange("p (c i) t -> p c t i", i=4),
                    in_=raw[:, :, VECTOR_COLUMNS:PIECE].rearrange("p t (c i) -> p c t i", i=4),
                )
                weight_grouped[(c, piece)] = grouped

        def quantise_weights(c):
            for piece in range(FEAT // PIECE):
                columns = slice(piece * PIECE, (piece + 1) * PIECE)
                nc.vector.quantize_mx(
                    out=weight_codes[:, c, columns].bitcast(FP8X4),
                    scales=weight_scales[:, c, columns],
                    in_=weight_grouped[(c, piece)][:].rearrange("p m t -> p (m t)"),
                )

        def first_layer_product(first_pass, codes, scales, first_unit, width):
            groups = BANK // width
            acc = psum.tile([P, groups, width], F32, tag="bank", name="acc1")
            for j in range(groups):
                units = slice(first_unit + j * P, first_unit + (j + 1) * P)
                for g in range(PASSES):
                    rows = slice(g * width, (g + 1) * width)
                    nc.tensor.matmul_mx(
                        out=acc[:, j, :],
                        lhsT=weight_codes[:, first_pass + g, units].bitcast(FP8X4),
                        lhsT_scale=weight_scales[:, first_pass + g, units],
                        rhs=codes[:, rows].bitcast(FP8X4),
                        rhs_scale=scales[:, rows],
                        start=(g == 0),
                        stop=(g == PASSES - 1),
                    )
            return acc

        edge_codes = keep.tile([P, BLOCKS // TURN, PASSES * TURN * P], U32, name="edge_codes", align_bytes=64)
        edge_scales = keep.tile([P, BLOCKS // TURN, PASSES * TURN * P], U8, name="edge_scales", align_bytes=64)
        edge_grouped = {}
        acc1 = {}
        hidden = {}
        hidden_codes = {}
        hidden_scales = {}
        acc2 = {}

        def turn_edges(b):
            grouped = stream.tile([P, TURN * FEAT], BF16, name="edge_grouped", align_bytes=64)
            words = grouped[:].bitcast(F32).rearrange("p (g b n u) -> p g b n u", g=PASSES, b=TURN, u=2)
            for i in range(TURN):
                turn_features(edge_raw[b][:, i, :], words[:, :, i, :, :])
            edge_grouped[b] = grouped

        def quantise_edges(b):
            nc.vector.quantize_mx(
                out=edge_codes[:, b // TURN, :].bitcast(FP8X4),
                scales=edge_scales[:, b // TURN, :],
                in_=edge_grouped[b][:],
            )

        def first_layer_matmuls(k):
            pair, h = divmod(k, 2)
            acc1[k] = [
                first_layer_product(
                    PASSES, edge_codes[:, pair, :], edge_scales[:, pair, :], h * K_PASS + q * 2 * P, TURN * P
                )
                for q in range(2)
            ]

        def first_layer_gelu(k):
            h = k % 2
            pre = stream.tile([P, 2, TURN, P, 2], F32, name="pre1")
            hid = stream.tile([P, TURN * P, PACK], BF16, name="hidden", align_bytes=64)
            for q in range(2):
                nc.vector.tensor_tensor(
                    out=pre[:, q, :, :, :],
                    in0=acc1[k][q][:].rearrange("p j (b n) -> p b n j", b=TURN),
                    in1=node_term[:, h, q, :, :].unsqueeze(1).to_broadcast([P, TURN, P, 2]),
                    op=ADD,
                )
            nc.scalar.activation(
                out=hid[:].rearrange("p r (q j) -> p r q j", q=2),
                in_=pre[:].rearrange("p q b n j -> p (b n) q j"),
                func=GELU,
            )
            hidden[k] = hid

        def quantise_hidden(k):
            codes = waiting.tile([P, TURN * P], U32, name="hidden_codes", align_bytes=64)
            scales = waiting.tile([P, TURN * P], U8, name="hidden_scales", align_bytes=64)
            nc.vector.quantize_mx(
                out=codes[:].bitcast(FP8X4), scales=scales[:], in_=hidden[k][:].rearrange("p r j -> p (r j)")
            )
            hidden_codes[k] = codes
            hidden_scales[k] = scales

        def second_layer_matmuls(b):
            acc2[b] = []
            pair, i = divmod(b, TURN)
            rows = slice(i * P, (i + 1) * P)
            for f in range(FEAT // BANK):
                acc = psum.tile([P, BANK], F32, tag="bank", name="acc2")
                for h in range(PASSES):
                    nc.tensor.matmul_mx(
                        out=acc[:],
                        lhsT=hidden_codes[2 * pair + h][:, rows].bitcast(FP8X4),
                        lhsT_scale=hidden_scales[2 * pair + h][:, rows],
                        rhs=weight_codes[:, 2 * PASSES + h, f * BANK : (f + 1) * BANK].bitcast(FP8X4),
                        rhs_scale=weight_scales[:, 2 * PASSES + h, f * BANK : (f + 1) * BANK],
                        start=(h == 0),
                        stop=(h == PASSES - 1),
                    )
                acc2[b].append(acc)

        def second_layer_gelu_and_store(b):
            pre = stream.tile([P, FEAT], F32, name="pre2")
            result = stream.tile([P, FEAT], F32, name="result")
            width = BANK // 2 if b == BLOCKS - 1 else BANK
            for m in range(0, FEAT, width):
                f, start = divmod(m, BANK)
                units = slice(m, m + width)
                nc.vector.tensor_tensor(
                    out=pre[:, units], in0=acc2[b][f][:, start : start + width], in1=bias2[:, units], op=ADD
                )
                nc.scalar.activation(out=result[:, units], in_=pre[:, units], func=GELU)
                nc.sync.dma_start(out=out_rows[:, b, units], in_=result[:, units])

        regroup_weights(0)
        turn_edges(0)

        node_grouped = keep.tile([P, FEAT], BF16, name="node_grouped", align_bytes=64)
        node_codes = keep.tile([P, PASSES * P], U32, name="node_codes", align_bytes=64)
        node_scales = keep.tile([P, PASSES * P], U8, name="node_scales", align_bytes=64)
        turn_features(
            node_raw[:], node_grouped[:].bitcast(F32).rearrange("p (g n u) -> p g n u", g=PASSES, u=2)
        )

        bias1_rows_f32 = keep.tile([P, P], F32, name="bias1_rows_f32")
        nc.vector.tensor_copy(out=bias1_rows_f32[:], in_=bias1_rows[:])
        bias1_turned = psum.tile([P, P], F32, tag="bank", name="bias1_turned")
        nc.tensor.transpose(bias1_turned[:], bias1_rows_f32[:], ident[:])
        bias1 = keep.tile([P, FEAT // P], F32, name="bias1")
        nc.vector.tensor_copy(out=bias1[:], in_=bias1_turned[:, 0 : FEAT // P])

        bias2 = keep.tile([P, FEAT], F32, name="bias2")
        for f in range(FEAT // BANK):
            units = slice(f * BANK, (f + 1) * BANK)
            spread = psum.tile([P, BANK], F32, tag="bank", name="spread")
            nc.tensor.matmul(out=spread[:], lhsT=ones[:], rhs=bias2_row[:, units], start=True, stop=True)
            nc.scalar.copy(out=bias2[:, units], in_=spread[:])

        quantise_edges(0)
        nc.vector.quantize_mx(out=node_codes[:].bitcast(FP8X4), scales=node_scales[:], in_=node_grouped[:])

        for c in range(1, 2 * PASSES):
            regroup_weights(c)
            quantise_weights(c - 1)
        quantise_weights(2 * PASSES - 1)

        node_term = keep.tile([P, PASSES, 2, P, 2], F32, name="node_term")
        for h in range(PASSES):
            acc = first_layer_product(0, node_codes[:], node_scales[:], h * K_PASS, P)
            bias = bias1[:, h * PACK : (h + 1) * PACK].rearrange("p (q j) -> p q j", q=2)
            nc.vector.tensor_tensor(
                out=node_term[:, h, :, :, :],
                in0=acc[:].rearrange("p (q j) n -> p q n j", q=2),
                in1=bias.unsqueeze(2).to_broadcast([P, 2, P, 2]),
                op=ADD,
            )

        def live(b):
            return 0 <= b < BLOCKS

        for step in range(-1, BLOCKS + LAG + 1):
            turning = step + LEAD
            turns = TURN <= turning < BLOCKS and turning % TURN == 0
            if turns:
                turn_edges(turning)
            if live(step + 1):
                first_layer_matmuls(step + 1)
            if live(step):
                first_layer_gelu(step)
            if turns:
                quantise_edges(turning)
            if 0 <= step < PASSES:
                regroup_weights(2 * PASSES + step)
            if 1 <= step <= PASSES:
                quantise_weights(2 * PASSES + step - 1)
            if live(step - 1):
                quantise_hidden(step - 1)
            if live(step - LAG):
                second_layer_matmuls(step - LAG)
            if live(step - LAG - 1):
                second_layer_gelu_and_store(step - LAG - 1)
